import numpy as np
import ml_dtypes


def mxq(x, axis, fmt="e4m3"):
    dtype, down = {"e4m3": (ml_dtypes.float8_e4m3fn, 7), "e5m2": (ml_dtypes.float8_e5m2, 14)}[fmt]
    v = np.moveaxis(np.asarray(x, np.float32).astype(ml_dtypes.bfloat16).astype(np.float64), axis, -1)
    blocks = v.reshape(v.shape[:-1] + (-1, 32))
    amax = np.abs(blocks).max(-1, keepdims=True)
    byte = np.maximum(np.where(amax > 0, np.frexp(amax)[1] - 1 + 127, 0) - down, 1)
    scale = np.exp2(byte - 127.0)
    codes = (blocks / scale).astype(np.float32).astype(dtype).astype(np.float64)
    return np.moveaxis((codes * scale).reshape(v.shape), -1, axis)


WIDE = False


def mx_kscale(k):
    if not WIDE:
        return np.ones(k)
    levels = np.array([10, -10, 5, -5, 0])
    a = np.random.permutation(np.resize(levels, k // 512 * 4)).reshape(k // 512, 4)
    idx = np.arange(k)
    return np.exp2(a[idx // 512, idx % 128 // 32])


BF16 = ml_dtypes.bfloat16


def bf(x):
    return np.asarray(x, np.float32).astype(BF16)


def f64(x):
    return np.asarray(x).astype(np.float64)


N, D, HOP = 4096, 128, 2
NW = HOP + 1


def setup_inputs():
    s = mx_kscale(N)
    u = s / s.min()
    g = u[None, :] / u[:, None]
    return {"A_p": bf(np.random.standard_normal((N, N)) / np.sqrt(N) * g),
            "x_p": bf(np.random.standard_normal((N, D)) / u[:, None]),
            "w_p": bf(1.0 + 0.1 * np.random.standard_normal((NW, 1)))}


def reference(A_p, x_p, w_p):
    ap = mxq(f64(A_p), 1, "e4m3")
    x = f64(x_p)
    wa, wb, wc = f64(w_p)
    feat_p = wa * x
    h1 = ap @ mxq(x, 0, "e4m3")
    feat_p = feat_p + wb * h1
    feat_p = feat_p + wc * (ap @ mxq(h1, 0, "e4m3"))
    return feat_p

@@ -1,0 +1,241 @@
+from contextlib import ExitStack
+
+import concourse.masks as masks
+import concourse.mybir as mybir
+
+F32 = mybir.dt.float32
+BF16 = mybir.dt.bfloat16
+U32 = mybir.dt.uint32
+U8 = mybir.dt.uint8
+FP8X4 = mybir.dt.float8_e4m3fn_x4
+ALU = mybir.AluOpType
+ACT = mybir.ActivationFunctionType
+
+P = 128
+N = 4096
+D = 128
+UNITS = 16
+PASSES = 8
+FLOPS = 2 * 2 * N * N * D
+
+VECTOR_DRAINS = ((0, 3), (1, 1), (1, 5))
+TRICK = True
+
+
+def tile_simpa_pb_t_kernel(tc, A_p, x_p, w_p, out):
+    nc = tc.nc
+    a_units = A_p.rearrange("(j m e) k -> j m (e k)", m=P, e=2)
+    out_groups = out.rearrange("(g u m e) d -> g m u (e d)", g=PASSES, u=2, m=P, e=2)
+
+    with ExitStack() as ctx:
+        keep = ctx.enter_context(tc.tile_pool(name="keep", bufs=1))
+        rawp = ctx.enter_context(tc.tile_pool(name="rawp", bufs=3))
+        grpp = ctx.enter_context(tc.tile_pool(name="grpp", bufs=4))
+        h1gp = ctx.enter_context(tc.tile_pool(name="h1gp", bufs=2))
+        tpp = ctx.enter_context(tc.psum_pool(name="tpp", bufs=6))
+        hpp = ctx.enter_context(tc.psum_pool(name="hpp", bufs=2))
+        ctx.enter_context(tc.manual_schedule())
+
+        a_codes = keep.tile([P, 32 * 1024], U32, name="a_codes", align_bytes=64)
+        a_scales = keep.tile([P, 8 * 1024], U8, name="a_scales", align_bytes=64)
+        xh_codes = keep.tile([P, PASSES * 256], U32, name="xh_codes", align_bytes=64)
+        xh_scales = keep.tile([P, PASSES * 256], U8, name="xh_scales", align_bytes=64)
+        feat = keep.tile([P, 32 * D], F32, name="feat")
+        ident = keep.tile([P, P], F32, name="ident")
+        w_bf = keep.tile([P, 3], BF16, name="w_bf")
+        w_f = keep.tile([P, 3], F32, name="w_f")
+
+        raws = {}
+        hps = {}
+        h1gs = {}
+        pending = []
+        quantised = [0]
+
+        def avail(j):
+            return j // 2 if TRICK else 0
+
+        def a_plane(r, lo, width):
+            g = r // 4
+            rho = (g // 4) * 4 + r % 4
+            k = 4 * (g % 4)
+            return a_scales[k:P, rho * 1024 + lo : rho * 1024 + lo + width]
+
+        def load(j):
+            raw = rawp.tile([P, 2 * N], BF16, tag="raw", name="raw")
+            raws[j] = raw
+            if j == 0 or j == UNITS - 1:
+                for e in range(2):
+                    nc.sync.dma_start(out=raw[:, e * N : (e + 1) * N], in_=a_units[j][:, e * N : (e + 1) * N])
+            else:
+                nc.sync.dma_start(out=raw[:], in_=a_units[j])
+
+        def quantise_next():
+            grp, j, h = pending[quantised[0]]
+            quantised[0] += 1
+            r = 2 * j + h // 2
+            lo = (h % 2) * 512
+            nc.vector.quantize_mx(
+                out=a_codes[:, r * 1024 + lo : r * 1024 + lo + 512].bitcast(FP8X4),
+                scales=a_plane(r, lo, 512),
+                in_=grp[:],
+            )
+
+        def hop1(j, e):
+            if e == 0:
+                hps[j] = hpp.tile([P, 512], F32, tag="hp", name="hp")
+            hp = hps[j]
+            r = 2 * j + e
+            for c in range(PASSES):
+                n = 256 if c < avail(j) else 128
+                nc.tensor.matmul_mx(
+                    out=hp[:, e * 256 : e * 256 + n],
+                    lhsT=a_codes[:, r * 1024 + c * 128 : r * 1024 + (c + 1) * 128].bitcast(FP8X4),
+                    lhsT_scale=a_plane(r, c * 128, 128),
+                    rhs=xh_codes[:, c * 256 : c * 256 + n].bitcast(FP8X4),
+                    rhs_scale=xh_scales[:, c * 256 : c * 256 + n],
+                    start=(c == 0),
+                    stop=(c == PASSES - 1),
+                )
+
+        def round_h1(j):
+            g = j // 2
+            u = j % 2
+            if u == 0:
+                h1gs[g] = h1gp.tile([P, 4 * D], BF16, tag="h1g", name="h1g", align_bytes=64)
+            parts = hps[j][:].rearrange("p (e s d) -> p e s d", e=2, s=2)
+            nc.scalar.copy(
+                out=h1gs[g][:].rearrange("p (d t) -> p d t", t=4)[:, :, 2 * u : 2 * u + 2],
+                in_=parts[:, :, 0, :].rearrange("p e d -> p d e"),
+            )
+
+        def add_to_feat(j):
+            parts = hps[j][:].rearrange("p (e s d) -> p e s d", e=2, s=2)
+            fv = feat[:, 2 * j * D : (2 * j + 2) * D].rearrange("p (e d) -> p e d", e=2)
+            nc.vector.scalar_tensor_tensor(
+                out=fv, in0=parts[:, :, 0, :], scalar=w_f[:, 1:2], in1=fv, op0=ALU.mult, op1=ALU.add
+            )
+            if avail(j) > 0:
+                nc.vector.scalar_tensor_tensor(
+                    out=fv, in0=parts[:, :, 1, :], scalar=w_f[:, 2:3], in1=fv, op0=ALU.mult, op1=ALU.add
+                )
+
+        def quantise_h1(g):
+            nc.vector.quantize_mx(
+                out=xh_codes[:, g * 256 + 128 : g * 256 + 256].bitcast(FP8X4),
+                scales=xh_scales[:, g * 256 + 128 : g * 256 + 256],
+                in_=h1gs[g][:],
+            )
+
+        def transposes(j):
+            rawf = raws[j][:].bitcast(F32)
+            grp = None
+            for b in range(8):
+                pt = tpp.tile([P, 512], F32, tag="tp", name="pt")
+                for q in range(4):
+                    lo = b * 512 + q * 128
+                    nc.tensor.transpose(out=pt[:, q * 128 : (q + 1) * 128], in_=rawf[:, lo : lo + 128], identity=ident[:])
+                if b % 2 == 0:
+                    grp = grpp.tile([P, 2048], BF16, tag="grp", name="grp", align_bytes=64)
+                dst = grp[:].bitcast(F32)[:, (b % 2) * 512 : (b % 2 + 1) * 512].rearrange("p (c m u) -> p c m u", c=2, u=2)
+                src = pt[:].rearrange("p (c u m) -> p c m u", c=2, u=2)
+                if (j % 2, b) in VECTOR_DRAINS:
+                    nc.vector.tensor_copy(out=dst, in_=src)
+                else:
+                    nc.scalar.copy(out=dst, in_=src)
+                if b % 2 == 1:
+                    pending.append((grp, j, b // 2))
+                    if len(pending) - quantised[0] > 1:
+                        quantise_next()
+                if b == 2 and j >= 2:
+                    round_h1(j - 2)
+                    add_to_feat(j - 2)
+                if b == 4 and j >= 3 and j % 2 == 1:
+                    quantise_h1((j - 2) // 2)
+
+        nc.scalar.dma_start(out=w_bf[:], in_=w_p.rearrange("a b -> (a b)").partition_broadcast(P))
+        x_raw = rawp.tile([P, 32 * D], BF16, tag="raw", name="x_raw")
+        nc.sync.dma_start(
+            out=x_raw[:].rearrange("p (j w) -> p j w", j=UNITS),
+            in_=x_p.rearrange("(j m e) d -> m j (e d)", m=P, e=2),
+        )
+        load(0)
+        load(1)
+        masks.make_identity(nc, ident[:])
+        nc.vector.tensor_copy(out=w_f[:], in_=w_bf[:])
+        xgs = []
+        for h in range(2):
+            xg = grpp.tile([P, 2048], BF16, tag="grp", name="xg", align_bytes=64)
+            xgs.append(xg)
+            nc.vector.tensor_copy(
+                out=xg[:].rearrange("p (c d t) -> p c d t", c=4, t=4),
+                in_=x_raw[:, h * 2048 : (h + 1) * 2048].rearrange("p (c t d) -> p c d t", c=4, t=4),
+            )
+        for c in range(PASSES):
+            nc.vector.quantize_mx(
+                out=xh_codes[:, c * 256 : c * 256 + 128].bitcast(FP8X4),
+                scales=xh_scales[:, c * 256 : c * 256 + 128],
+                in_=xgs[c // 4][:, (c % 4) * 512 : (c % 4 + 1) * 512],
+            )
+        for h in range(4):
+            nc.scalar.activation(
+                out=feat[:, h * 1024 : (h + 1) * 1024],
+                in_=x_raw[:, h * 1024 : (h + 1) * 1024],
+                func=ACT.Copy,
+                scale=w_f[:, 0:1],
+            )
+
+        for j in range(UNITS):
+            if j + 2 < UNITS:
+                load(j + 2)
+            transposes(j)
+            if j >= 1:
+                hop1(j - 1, 0)
+                hop1(j - 1, 1)
+        while len(pending) > quantised[0]:
+            quantise_next()
+
+        tails = {}
+
+        def tail_passes(g, t, first, last):
+            if g not in tails:
+                if g < 6:
+                    tails[g] = tpp.tile([P, 512], F32, tag="tp", name="tl")
+                else:
+                    tails[g] = hpp.tile([P, 512], F32, tag="hp", name="tl")
+            r = 4 * g + t
+            for c in range(first, last + 1):
+                nc.tensor.matmul_mx(
+                    out=tails[g][:, t * 128 : (t + 1) * 128],
+                    lhsT=a_codes[:, r * 1024 + c * 128 : r * 1024 + (c + 1) * 128].bitcast(FP8X4),
+                    lhsT_scale=a_plane(r, c * 128, 128),
+                    rhs=xh_codes[:, c * 256 + 128 : c * 256 + 256].bitcast(FP8X4),
+                    rhs_scale=xh_scales[:, c * 256 + 128 : c * 256 + 256],
+                    start=(c == avail(r // 2)),
+                    stop=(c == PASSES - 1),
+                )
+
+        last = UNITS - 1
+        round_h1(last - 1)
+        add_to_feat(last - 1)
+        for g in (0, 1):
+            tail_passes(g, 0, avail(2 * g), PASSES - 2)
+        hop1(last, 0)
+        for g in (2, 3):
+            tail_passes(g, 0, avail(2 * g), PASSES - 2)
+        hop1(last, 1)
+        for g in (4, 5):
+            tail_passes(g, 0, avail(2 * g), PASSES - 2)
+        round_h1(last)
+        quantise_h1(PASSES - 1)
+        add_to_feat(last)
+        for g in range(PASSES):
+            for t in range(4):
+                if t == 0 and g < 6:
+                    tail_passes(g, 0, PASSES - 1, PASSES - 1)
+                else:
+                    tail_passes(g, t, avail(2 * g), PASSES - 1)
+            fv = feat[:, g * 512 : (g + 1) * 512]
+            nc.vector.scalar_tensor_tensor(
+                out=fv, in0=tails[g][:], scalar=w_f[:, 2:3], in1=fv, op0=ALU.mult, op1=ALU.add
+            )
+            nc.sync.dma_start(out=out_groups[g], in_=fv.rearrange("p (u w) -> p u w", u=2))

@@ -15,11 +15,9 @@ P = 128
 N = 4096
 D = 128
 UNITS = 16
+TILES = 32
 PASSES = 8
 FLOPS = 2 * 2 * N * N * D
-
-VECTOR_DRAINS = ((0, 3), (1, 1), (1, 5))
-TRICK = True
 
 
 def tile_simpa_pb_t_kernel(tc, A_p, x_p, w_p, out):
@@ -36,11 +34,11 @@ def tile_simpa_pb_t_kernel(tc, A_p, x_p, w_p, out):
         hpp = ctx.enter_context(tc.psum_pool(name="hpp", bufs=2))
         ctx.enter_context(tc.manual_schedule())
 
-        a_codes = keep.tile([P, 32 * 1024], U32, name="a_codes", align_bytes=64)
+        a_codes = keep.tile([P, TILES * 1024], U32, name="a_codes", align_bytes=64)
         a_scales = keep.tile([P, 8 * 1024], U8, name="a_scales", align_bytes=64)
         xh_codes = keep.tile([P, PASSES * 256], U32, name="xh_codes", align_bytes=64)
         xh_scales = keep.tile([P, PASSES * 256], U8, name="xh_scales", align_bytes=64)
-        feat = keep.tile([P, 32 * D], F32, name="feat")
+        feat = keep.tile([P, TILES * D], F32, name="feat")
         ident = keep.tile([P, P], F32, name="ident")
         w_bf = keep.tile([P, 3], BF16, name="w_bf")
         w_f = keep.tile([P, 3], F32, name="w_f")
@@ -51,8 +49,8 @@ def tile_simpa_pb_t_kernel(tc, A_p, x_p, w_p, out):
         pending = []
         quantised = [0]
 
-        def avail(j):
-            return j // 2 if TRICK else 0
+        def avail(r):
+            return max(0, (r - 2) // 4)
 
         def a_plane(r, lo, width):
             g = r // 4
@@ -70,32 +68,34 @@ def tile_simpa_pb_t_kernel(tc, A_p, x_p, w_p, out):
                 nc.sync.dma_start(out=raw[:], in_=a_units[j])
 
         def quantise_next():
-            grp, j, h = pending[quantised[0]]
+            grp, r, h = pending[quantised[0]]
             quantised[0] += 1
-            r = 2 * j + h // 2
-            lo = (h % 2) * 512
+            lo = r * 1024 + h * 512
             nc.vector.quantize_mx(
-                out=a_codes[:, r * 1024 + lo : r * 1024 + lo + 512].bitcast(FP8X4),
-                scales=a_plane(r, lo, 512),
+                out=a_codes[:, lo : lo + 512].bitcast(FP8X4),
+                scales=a_plane(r, h * 512, 512),
                 in_=grp[:],
             )
 
-        def hop1(j, e):
+        def mx_pass(acc, r, c, lo, n, start):
+            nc.tensor.matmul_mx(
+                out=acc,
+                lhsT=a_codes[:, r * 1024 + c * 128 : r * 1024 + (c + 1) * 128].bitcast(FP8X4),
+                lhsT_scale=a_plane(r, c * 128, 128),
+                rhs=xh_codes[:, c * 256 + lo : c * 256 + lo + n].bitcast(FP8X4),
+                rhs_scale=xh_scales[:, c * 256 + lo : c * 256 + lo + n],
+                start=start,
+                stop=(c == PASSES - 1),
+            )
+
+        def hop1(r):
+            j = r // 2
+            e = r % 2
             if e == 0:
                 hps[j] = hpp.tile([P, 512], F32, tag="hp", name="hp")
-            hp = hps[j]
-            r = 2 * j + e
             for c in range(PASSES):
-                n = 256 if c < avail(j) else 128
-                nc.tensor.matmul_mx(
-                    out=hp[:, e * 256 : e * 256 + n],
-                    lhsT=a_codes[:, r * 1024 + c * 128 : r * 1024 + (c + 1) * 128].bitcast(FP8X4),
-                    lhsT_scale=a_plane(r, c * 128, 128),
-                    rhs=xh_codes[:, c * 256 : c * 256 + n].bitcast(FP8X4),
-                    rhs_scale=xh_scales[:, c * 256 : c * 256 + n],
-                    start=(c == 0),
-                    stop=(c == PASSES - 1),
-                )
+                n = 256 if c < avail(r) else 128
+                mx_pass(hps[j][:, e * 256 : e * 256 + n], r, c, 0, n, c == 0)
 
         def round_h1(j):
             g = j // 2
@@ -114,7 +114,7 @@ def tile_simpa_pb_t_kernel(tc, A_p, x_p, w_p, out):
             nc.vector.scalar_tensor_tensor(
                 out=fv, in0=parts[:, :, 0, :], scalar=w_f[:, 1:2], in1=fv, op0=ALU.mult, op1=ALU.add
             )
-            if avail(j) > 0:
+            if avail(2 * j) > 0:
                 nc.vector.scalar_tensor_tensor(
                     out=fv, in0=parts[:, :, 1, :], scalar=w_f[:, 2:3], in1=fv, op0=ALU.mult, op1=ALU.add
                 )
@@ -126,34 +126,34 @@ def tile_simpa_pb_t_kernel(tc, A_p, x_p, w_p, out):
                 in_=h1gs[g][:],
             )
 
-        def transposes(j):
-            rawf = raws[j][:].bitcast(F32)
+        def transposes(r):
+            rawf = raws[r // 2][:].bitcast(F32)
             grp = None
-            for b in range(8):
+            for b in range(4):
                 pt = tpp.tile([P, 512], F32, tag="tp", name="pt")
                 for q in range(4):
-                    lo = b * 512 + q * 128
+                    lo = (r % 2) * 2048 + b * 512 + q * 128
                     nc.tensor.transpose(out=pt[:, q * 128 : (q + 1) * 128], in_=rawf[:, lo : lo + 128], identity=ident[:])
                 if b % 2 == 0:
                     grp = grpp.tile([P, 2048], BF16, tag="grp", name="grp", align_bytes=64)
                 dst = grp[:].bitcast(F32)[:, (b % 2) * 512 : (b % 2 + 1) * 512].rearrange("p (c m u) -> p c m u", c=2, u=2)
                 src = pt[:].rearrange("p (c u m) -> p c m u", c=2, u=2)
-                if (j % 2, b) in VECTOR_DRAINS:
+                if b == 3 and r % 4 != 3:
                     nc.vector.tensor_copy(out=dst, in_=src)
                 else:
                     nc.scalar.copy(out=dst, in_=src)
                 if b % 2 == 1:
-                    pending.append((grp, j, b // 2))
+                    pending.append((grp, r, b // 2))
                     if len(pending) - quantised[0] > 1:
                         quantise_next()
-                if b == 2 and j >= 2:
-                    round_h1(j - 2)
-                    add_to_feat(j - 2)
-                if b == 4 and j >= 3 and j % 2 == 1:
-                    quantise_h1((j - 2) // 2)
+                if b == 1 and r % 2 == 0 and r >= 4:
+                    round_h1((r - 4) // 2)
+                    add_to_feat((r - 4) // 2)
+                if b == 3 and r % 4 == 2 and r >= 6:
+                    quantise_h1((r - 6) // 4)
 
         nc.scalar.dma_start(out=w_bf[:], in_=w_p.rearrange("a b -> (a b)").partition_broadcast(P))
-        x_raw = rawp.tile([P, 32 * D], BF16, tag="raw", name="x_raw")
+        x_raw = rawp.tile([P, TILES * D], BF16, tag="raw", name="x_raw")
         nc.sync.dma_start(
             out=x_raw[:].rearrange("p (j w) -> p j w", j=UNITS),
             in_=x_p.rearrange("(j m e) d -> m j (e d)", m=P, e=2),
@@ -184,56 +184,44 @@ def tile_simpa_pb_t_kernel(tc, A_p, x_p, w_p, out):
                 scale=w_f[:, 0:1],
             )
 
-        for j in range(UNITS):
-            if j + 2 < UNITS:
-                load(j + 2)
-            transposes(j)
-            if j >= 1:
-                hop1(j - 1, 0)
-                hop1(j - 1, 1)
+        for r in range(TILES):
+            if r % 2 == 0 and r // 2 + 2 < UNITS:
+                load(r // 2 + 2)
+            transposes(r)
+            if r >= 2:
+                hop1(r - 2)
         while len(pending) > quantised[0]:
             quantise_next()
 
         tails = {}
 
-        def tail_passes(g, t, first, last):
+        def tail_passes(g, t, first, final):
             if g not in tails:
                 if g < 6:
                     tails[g] = tpp.tile([P, 512], F32, tag="tp", name="tl")
                 else:
                     tails[g] = hpp.tile([P, 512], F32, tag="hp", name="tl")
             r = 4 * g + t
-            for c in range(first, last + 1):
-                nc.tensor.matmul_mx(
-                    out=tails[g][:, t * 128 : (t + 1) * 128],
-                    lhsT=a_codes[:, r * 1024 + c * 128 : r * 1024 + (c + 1) * 128].bitcast(FP8X4),
-                    lhsT_scale=a_plane(r, c * 128, 128),
-                    rhs=xh_codes[:, c * 256 + 128 : c * 256 + 256].bitcast(FP8X4),
-                    rhs_scale=xh_scales[:, c * 256 + 128 : c * 256 + 256],
-                    start=(c == avail(r // 2)),
-                    stop=(c == PASSES - 1),
-                )
+            for c in range(first, final + 1):
+                mx_pass(tails[g][:, t * 128 : (t + 1) * 128], r, c, 128, 128, c == avail(r))
 
-        last = UNITS - 1
-        round_h1(last - 1)
-        add_to_feat(last - 1)
-        for g in (0, 1):
-            tail_passes(g, 0, avail(2 * g), PASSES - 2)
-        hop1(last, 0)
-        for g in (2, 3):
-            tail_passes(g, 0, avail(2 * g), PASSES - 2)
-        hop1(last, 1)
-        for g in (4, 5):
-            tail_passes(g, 0, avail(2 * g), PASSES - 2)
-        round_h1(last)
+        round_h1(UNITS - 2)
+        add_to_feat(UNITS - 2)
+        hop1(TILES - 2)
+        for g in (0, 1, 2):
+            tail_passes(g, 0, avail(4 * g), PASSES - 2)
+        hop1(TILES - 1)
+        for g in (3, 4, 5):
+            tail_passes(g, 0, avail(4 * g), PASSES - 2)
+        round_h1(UNITS - 1)
         quantise_h1(PASSES - 1)
-        add_to_feat(last)
+        add_to_feat(UNITS - 1)
         for g in range(PASSES):
             for t in range(4):
                 if t == 0 and g < 6:
                     tail_passes(g, 0, PASSES - 1, PASSES - 1)
                 else:
-                    tail_passes(g, t, avail(2 * g), PASSES - 1)
+                    tail_passes(g, t, avail(4 * g + t), PASSES - 1)
             fv = feat[:, g * 512 : (g + 1) * 512]
             nc.vector.scalar_tensor_tensor(
                 out=fv, in0=tails[g][:], scalar=w_f[:, 2:3], in1=fv, op0=ALU.mult, op1=ALU.add

@@ -16,8 +16,14 @@ N = 4096
 D = 128
 UNITS = 16
 TILES = 32
+BANKS = 128
 PASSES = 8
 FLOPS = 2 * 2 * N * N * D
+
+RUN = 4
+LAG = 16
+PREWARM = 20
+FILLER = True
 
 
 def tile_simpa_pb_t_kernel(tc, A_p, x_p, w_p, out):
@@ -42,15 +48,19 @@ def tile_simpa_pb_t_kernel(tc, A_p, x_p, w_p, out):
         ident = keep.tile([P, P], F32, name="ident")
         w_bf = keep.tile([P, 3], BF16, name="w_bf")
         w_f = keep.tile([P, 3], F32, name="w_f")
+        warm = keep.tile([P, 512], BF16, name="warm")
 
         raws = {}
         hps = {}
         h1gs = {}
-        pending = []
-        quantised = [0]
+        grps = {}
+        evacuate_at = {}
+        quantise_h1_at = {}
+        issued = [0]
+        h1_ready = [0]
 
         def avail(r):
-            return max(0, (r - 2) // 4)
+            return max(0, r // 4 - 1)
 
         def a_plane(r, lo, width):
             g = r // 4
@@ -67,14 +77,11 @@ def tile_simpa_pb_t_kernel(tc, A_p, x_p, w_p, out):
             else:
                 nc.sync.dma_start(out=raw[:], in_=a_units[j])
 
-        def quantise_next():
-            grp, r, h = pending[quantised[0]]
-            quantised[0] += 1
-            lo = r * 1024 + h * 512
+        def quantise_a(h):
             nc.vector.quantize_mx(
-                out=a_codes[:, lo : lo + 512].bitcast(FP8X4),
-                scales=a_plane(r, h * 512, 512),
-                in_=grp[:],
+                out=a_codes[:, h * 512 : (h + 1) * 512].bitcast(FP8X4),
+                scales=a_plane(h // 2, (h % 2) * 512, 512),
+                in_=grps[h][:],
             )
 
         def mx_pass(acc, r, c, lo, n, start):
@@ -88,14 +95,16 @@ def tile_simpa_pb_t_kernel(tc, A_p, x_p, w_p, out):
                 stop=(c == PASSES - 1),
             )
 
-        def hop1(r):
-            j = r // 2
-            e = r % 2
-            if e == 0:
-                hps[j] = hpp.tile([P, 512], F32, tag="hp", name="hp")
-            for c in range(PASSES):
+        def hop1_passes(upto):
+            while issued[0] < upto:
+                r = issued[0] // PASSES
+                c = issued[0] % PASSES
+                if r % 2 == 0 and c == 0:
+                    hps[r // 2] = hpp.tile([P, 512], F32, tag="hp", name="hp")
+                assert avail(r) <= h1_ready[0]
                 n = 256 if c < avail(r) else 128
-                mx_pass(hps[j][:, e * 256 : e * 256 + n], r, c, 0, n, c == 0)
+                mx_pass(hps[r // 2][:, (r % 2) * 256 : (r % 2) * 256 + n], r, c, 0, n, c == 0)
+                issued[0] += 1
 
         def round_h1(j):
             g = j // 2
@@ -125,33 +134,30 @@ def tile_simpa_pb_t_kernel(tc, A_p, x_p, w_p, out):
                 scales=xh_scales[:, g * 256 + 128 : g * 256 + 256],
                 in_=h1gs[g][:],
             )
+            h1_ready[0] += 1
 
-        def transposes(r):
-            rawf = raws[r // 2][:].bitcast(F32)
-            grp = None
-            for b in range(4):
-                pt = tpp.tile([P, 512], F32, tag="tp", name="pt")
-                for q in range(4):
-                    lo = (r % 2) * 2048 + b * 512 + q * 128
-                    nc.tensor.transpose(out=pt[:, q * 128 : (q + 1) * 128], in_=rawf[:, lo : lo + 128], identity=ident[:])
-                if b % 2 == 0:
-                    grp = grpp.tile([P, 2048], BF16, tag="grp", name="grp", align_bytes=64)
-                dst = grp[:].bitcast(F32)[:, (b % 2) * 512 : (b % 2 + 1) * 512].rearrange("p (c m u) -> p c m u", c=2, u=2)
-                src = pt[:].rearrange("p (c u m) -> p c m u", c=2, u=2)
-                if b == 3 and r % 4 != 3:
-                    nc.vector.tensor_copy(out=dst, in_=src)
-                else:
-                    nc.scalar.copy(out=dst, in_=src)
-                if b % 2 == 1:
-                    pending.append((grp, r, b // 2))
-                    if len(pending) - quantised[0] > 1:
-                        quantise_next()
-                if b == 1 and r % 2 == 0 and r >= 4:
-                    round_h1((r - 4) // 2)
-                    add_to_feat((r - 4) // 2)
-                if b == 3 and r % 4 == 2 and r >= 6:
-                    quantise_h1((r - 6) // 4)
+        def idle_work(count):
+            for i in range(count):
+                nc.tensor.matmul(out=wp[:], lhsT=warm[:, 0:P], rhs=warm[:], start=True, stop=True)
 
+        def transpose_bank(s):
+            rawf = raws[s // 8][:].bitcast(F32)
+            pt = tpp.tile([P, 512], F32, tag="tp", name="pt")
+            for q in range(4):
+                lo = (s % 8) * 512 + q * 128
+                nc.tensor.transpose(out=pt[:, q * 128 : (q + 1) * 128], in_=rawf[:, lo : lo + 128], identity=ident[:])
+            if s % 2 == 0:
+                grps[s // 2] = grpp.tile([P, 2048], BF16, tag="grp", name="grp", align_bytes=64)
+            dst = grps[s // 2][:].bitcast(F32)[:, (s % 2) * 512 : (s % 2 + 1) * 512].rearrange("p (c m u) -> p c m u", c=2, u=2)
+            src = pt[:].rearrange("p (c u m) -> p c m u", c=2, u=2)
+            if s % 4 == 3 and s % 16 != 15:
+                nc.vector.tensor_copy(out=dst, in_=src)
+            else:
+                nc.scalar.copy(out=dst, in_=src)
+
+        nc.vector.memset(warm[:], 0.0)
+        wp = hpp.tile([P, 512], F32, tag="hp", name="wp")
+        idle_work(PREWARM)
         nc.scalar.dma_start(out=w_bf[:], in_=w_p.rearrange("a b -> (a b)").partition_broadcast(P))
         x_raw = rawp.tile([P, TILES * D], BF16, tag="raw", name="x_raw")
         nc.sync.dma_start(
@@ -184,14 +190,28 @@ def tile_simpa_pb_t_kernel(tc, A_p, x_p, w_p, out):
                 scale=w_f[:, 0:1],
             )
 
-        for r in range(TILES):
-            if r % 2 == 0 and r // 2 + 2 < UNITS:
-                load(r // 2 + 2)
-            transposes(r)
-            if r >= 2:
-                hop1(r - 2)
-        while len(pending) > quantised[0]:
-            quantise_next()
+        for s in range(BANKS):
+            if s % 8 == 0 and s // 8 + 2 < UNITS:
+                load(s // 8 + 2)
+            transpose_bank(s)
+            if s % 2 == 1 and s >= 3:
+                quantise_a(s // 2 - 1)
+            if s in evacuate_at:
+                round_h1(evacuate_at[s])
+                add_to_feat(evacuate_at[s])
+            if s in quantise_h1_at:
+                quantise_h1(quantise_h1_at[s])
+            if (s + 1) % RUN == 0 or s == BANKS - 1:
+                before = issued[0]
+                hop1_passes(2 * (s + 1) - LAG)
+                if FILLER and s < BANKS - 1:
+                    idle_work((2 * RUN - (issued[0] - before)) // 4)
+                if issued[0] // 16 > before // 16:
+                    j = issued[0] // 16 - 1
+                    evacuate_at[s + 2] = j
+                    if j % 2 == 1:
+                        quantise_h1_at[s + 4] = j // 2
+        quantise_a(BANKS // 2 - 1)
 
         tails = {}
 
@@ -207,10 +227,10 @@ def tile_simpa_pb_t_kernel(tc, A_p, x_p, w_p, out):
 
         round_h1(UNITS - 2)
         add_to_feat(UNITS - 2)
-        hop1(TILES - 2)
+        hop1_passes((TILES - 1) * PASSES)
         for g in (0, 1, 2):
             tail_passes(g, 0, avail(4 * g), PASSES - 2)
-        hop1(TILES - 1)
+        hop1_passes(TILES * PASSES)
         for g in (3, 4, 5):
             tail_passes(g, 0, avail(4 * g), PASSES - 2)
         round_h1(UNITS - 1)

@@ -20,10 +20,8 @@ BANKS = 128
 PASSES = 8
 FLOPS = 2 * 2 * N * N * D
 
-RUN = 4
+RUN = 6
 LAG = 16
-PREWARM = 20
-FILLER = True
 
 
 def tile_simpa_pb_t_kernel(tc, A_p, x_p, w_p, out):
@@ -48,7 +46,6 @@ def tile_simpa_pb_t_kernel(tc, A_p, x_p, w_p, out):
         ident = keep.tile([P, P], F32, name="ident")
         w_bf = keep.tile([P, 3], BF16, name="w_bf")
         w_f = keep.tile([P, 3], F32, name="w_f")
-        warm = keep.tile([P, 512], BF16, name="warm")
 
         raws = {}
         hps = {}
@@ -136,10 +133,6 @@ def tile_simpa_pb_t_kernel(tc, A_p, x_p, w_p, out):
             )
             h1_ready[0] += 1
 
-        def idle_work(count):
-            for i in range(count):
-                nc.tensor.matmul(out=wp[:], lhsT=warm[:, 0:P], rhs=warm[:], start=True, stop=True)
-
         def transpose_bank(s):
             rawf = raws[s // 8][:].bitcast(F32)
             pt = tpp.tile([P, 512], F32, tag="tp", name="pt")
@@ -155,9 +148,6 @@ def tile_simpa_pb_t_kernel(tc, A_p, x_p, w_p, out):
             else:
                 nc.scalar.copy(out=dst, in_=src)
 
-        nc.vector.memset(warm[:], 0.0)
-        wp = hpp.tile([P, 512], F32, tag="hp", name="wp")
-        idle_work(PREWARM)
         nc.scalar.dma_start(out=w_bf[:], in_=w_p.rearrange("a b -> (a b)").partition_broadcast(P))
         x_raw = rawp.tile([P, TILES * D], BF16, tag="raw", name="x_raw")
         nc.sync.dma_start(
@@ -204,8 +194,6 @@ def tile_simpa_pb_t_kernel(tc, A_p, x_p, w_p, out):
             if (s + 1) % RUN == 0 or s == BANKS - 1:
                 before = issued[0]
                 hop1_passes(2 * (s + 1) - LAG)
-                if FILLER and s < BANKS - 1:
-                    idle_work((2 * RUN - (issued[0] - before)) // 4)
                 if issued[0] // 16 > before // 16:
                     j = issued[0] // 16 - 1
                     evacuate_at[s + 2] = j

@@ -12,226 +12,213 @@ ALU = mybir.AluOpType
 ACT = mybir.ActivationFunctionType
 
 P = 128
-N = 4096
-D = 128
-UNITS = 16
-TILES = 32
-BANKS = 128
-PASSES = 8
-FLOPS = 2 * 2 * N * N * D
+NODES = 4096
+FEATURES = 128
+PASSES = NODES // (4 * P)
+ROW_TILES = NODES // P
+PAIRS = ROW_TILES // 2
+BANK = 512
+TILE_WORDS = PASSES * P
+TRANSPOSE_BANKS = 6
+RAW_TILES = 6
+FLOPS = 2 * 2 * NODES * NODES * FEATURES
 
-RUN = 6
-LAG = 16
+
+def h1_groups_ready(r):
+    return max(0, (r - 2) // 4)
 
 
 def tile_simpa_pb_t_kernel(tc, A_p, x_p, w_p, out):
     nc = tc.nc
-    a_units = A_p.rearrange("(j m e) k -> j m (e k)", m=P, e=2)
-    out_groups = out.rearrange("(g u m e) d -> g m u (e d)", g=PASSES, u=2, m=P, e=2)
+    a_row_tiles = A_p.rearrange("(j m e) k -> j e m k", m=P, e=2)
+    out_groups = out.rearrange("(g u m e) d -> g m u (e d)", u=2, m=P, e=2)
 
     with ExitStack() as ctx:
         keep = ctx.enter_context(tc.tile_pool(name="keep", bufs=1))
-        rawp = ctx.enter_context(tc.tile_pool(name="rawp", bufs=3))
-        grpp = ctx.enter_context(tc.tile_pool(name="grpp", bufs=4))
-        h1gp = ctx.enter_context(tc.tile_pool(name="h1gp", bufs=2))
-        tpp = ctx.enter_context(tc.psum_pool(name="tpp", bufs=6))
-        hpp = ctx.enter_context(tc.psum_pool(name="hpp", bufs=2))
+        raw_pool = ctx.enter_context(tc.tile_pool(name="raw_pool", bufs=RAW_TILES))
+        grouped_pool = ctx.enter_context(tc.tile_pool(name="grouped_pool", bufs=4))
+        h1_pool = ctx.enter_context(tc.tile_pool(name="h1_pool", bufs=2))
+        transpose_psum = ctx.enter_context(tc.psum_pool(name="transpose_psum", bufs=TRANSPOSE_BANKS))
+        product_psum = ctx.enter_context(tc.psum_pool(name="product_psum", bufs=2))
         ctx.enter_context(tc.manual_schedule())
 
-        a_codes = keep.tile([P, TILES * 1024], U32, name="a_codes", align_bytes=64)
-        a_scales = keep.tile([P, 8 * 1024], U8, name="a_scales", align_bytes=64)
-        xh_codes = keep.tile([P, PASSES * 256], U32, name="xh_codes", align_bytes=64)
-        xh_scales = keep.tile([P, PASSES * 256], U8, name="xh_scales", align_bytes=64)
-        feat = keep.tile([P, TILES * D], F32, name="feat")
+        a_codes = keep.tile([P, ROW_TILES * TILE_WORDS], U32, name="a_codes", align_bytes=64)
+        a_scales = keep.tile([P, ROW_TILES // 4 * TILE_WORDS], U8, name="a_scales", align_bytes=64)
+        xh_codes = keep.tile([P, PASSES * 2 * FEATURES], U32, name="xh_codes", align_bytes=64)
+        xh_scales = keep.tile([P, PASSES * 2 * FEATURES], U8, name="xh_scales", align_bytes=64)
+        feat = keep.tile([P, ROW_TILES * FEATURES], F32, name="feat")
         ident = keep.tile([P, P], F32, name="ident")
-        w_bf = keep.tile([P, 3], BF16, name="w_bf")
-        w_f = keep.tile([P, 3], F32, name="w_f")
+        w_bf16 = keep.tile([P, 3], BF16, name="w_bf16")
+        w = keep.tile([P, 3], F32, name="w")
 
-        raws = {}
-        hps = {}
-        h1gs = {}
-        grps = {}
-        evacuate_at = {}
-        quantise_h1_at = {}
-        issued = [0]
-        h1_ready = [0]
+        raw = {}
+        grouped = {}
+        products = {}
+        h1_grouped = {}
+        hop2 = {}
 
-        def avail(r):
-            return max(0, r // 4 - 1)
-
-        def a_plane(r, lo, width):
+        def a_plane(r, first, width):
             g = r // 4
-            rho = (g // 4) * 4 + r % 4
-            k = 4 * (g % 4)
-            return a_scales[k:P, rho * 1024 + lo : rho * 1024 + lo + width]
+            columns = ((g // 4) * 4 + r % 4) * TILE_WORDS + first
+            return a_scales[4 * (g % 4) : P, columns : columns + width]
 
-        def load(j):
-            raw = rawp.tile([P, 2 * N], BF16, tag="raw", name="raw")
-            raws[j] = raw
-            if j == 0 or j == UNITS - 1:
-                for e in range(2):
-                    nc.sync.dma_start(out=raw[:, e * N : (e + 1) * N], in_=a_units[j][:, e * N : (e + 1) * N])
-            else:
-                nc.sync.dma_start(out=raw[:], in_=a_units[j])
+        def load(r):
+            raw[r] = raw_pool.tile([P, NODES], BF16, tag="raw", name="raw")
+            nc.sync.dma_start(out=raw[r][:], in_=a_row_tiles[r // 2][r % 2])
 
-        def quantise_a(h):
+        def quantise_a(r, half):
+            first = half * (TILE_WORDS // 2)
             nc.vector.quantize_mx(
-                out=a_codes[:, h * 512 : (h + 1) * 512].bitcast(FP8X4),
-                scales=a_plane(h // 2, (h % 2) * 512, 512),
-                in_=grps[h][:],
+                out=a_codes[:, r * TILE_WORDS + first : r * TILE_WORDS + first + TILE_WORDS // 2].bitcast(FP8X4),
+                scales=a_plane(r, first, TILE_WORDS // 2),
+                in_=grouped[(r, half)][:],
             )
 
-        def mx_pass(acc, r, c, lo, n, start):
+        def mx_pass(acc, r, c, first, width, start):
+            moving = slice(c * 2 * FEATURES + first, c * 2 * FEATURES + first + width)
             nc.tensor.matmul_mx(
                 out=acc,
-                lhsT=a_codes[:, r * 1024 + c * 128 : r * 1024 + (c + 1) * 128].bitcast(FP8X4),
-                lhsT_scale=a_plane(r, c * 128, 128),
-                rhs=xh_codes[:, c * 256 + lo : c * 256 + lo + n].bitcast(FP8X4),
-                rhs_scale=xh_scales[:, c * 256 + lo : c * 256 + lo + n],
+                lhsT=a_codes[:, r * TILE_WORDS + c * P : r * TILE_WORDS + (c + 1) * P].bitcast(FP8X4),
+                lhsT_scale=a_plane(r, c * P, P),
+                rhs=xh_codes[:, moving].bitcast(FP8X4),
+                rhs_scale=xh_scales[:, moving],
                 start=start,
                 stop=(c == PASSES - 1),
             )
 
-        def hop1_passes(upto):
-            while issued[0] < upto:
-                r = issued[0] // PASSES
-                c = issued[0] % PASSES
-                if r % 2 == 0 and c == 0:
-                    hps[r // 2] = hpp.tile([P, 512], F32, tag="hp", name="hp")
-                assert avail(r) <= h1_ready[0]
-                n = 256 if c < avail(r) else 128
-                mx_pass(hps[r // 2][:, (r % 2) * 256 : (r % 2) * 256 + n], r, c, 0, n, c == 0)
-                issued[0] += 1
+        def transposes(r):
+            words = raw[r][:].bitcast(F32)
+            for b in range(4):
+                bank = transpose_psum.tile([P, BANK], F32, tag="bank", name="bank")
+                for q in range(4):
+                    nc.tensor.transpose(
+                        out=bank[:, q * P : (q + 1) * P],
+                        in_=words[:, (4 * b + q) * P : (4 * b + q + 1) * P],
+                        identity=ident[:],
+                    )
+                half = b // 2
+                if b % 2 == 0:
+                    grouped[(r, half)] = grouped_pool.tile([P, 4 * BANK], BF16, tag="grouped", name="grouped", align_bytes=64)
+                target = grouped[(r, half)][:].bitcast(F32)[:, (b % 2) * BANK : (b % 2 + 1) * BANK]
+                target = target.rearrange("p (c m u) -> p c m u", c=2, u=2)
+                source = bank[:].rearrange("p (c u m) -> p c m u", c=2, u=2)
+                if b == 3 and r % 4 != 3:
+                    nc.vector.tensor_copy(out=target, in_=source)
+                else:
+                    nc.scalar.copy(out=target, in_=source)
+                if b == 1 and r > 0:
+                    quantise_a(r - 1, 1)
+                if b == 3:
+                    quantise_a(r, 0)
+                if b == 1 and r % 2 == 0 and r >= 4:
+                    round_h1((r - 4) // 2)
+                    add_products((r - 4) // 2)
+                if b == 3 and r % 4 == 2 and r >= 6:
+                    quantise_h1((r - 6) // 4)
 
-        def round_h1(j):
-            g = j // 2
-            u = j % 2
+        def hop1(r):
+            if r % 2 == 0:
+                products[r // 2] = product_psum.tile([P, BANK], F32, tag="products", name="products")
+            for c in range(PASSES):
+                width = 2 * FEATURES if c < h1_groups_ready(r) else FEATURES
+                first = (r % 2) * 2 * FEATURES
+                mx_pass(products[r // 2][:, first : first + width], r, c, 0, width, c == 0)
+
+        def round_h1(pair):
+            g = pair // 2
+            u = pair % 2
             if u == 0:
-                h1gs[g] = h1gp.tile([P, 4 * D], BF16, tag="h1g", name="h1g", align_bytes=64)
-            parts = hps[j][:].rearrange("p (e s d) -> p e s d", e=2, s=2)
+                h1_grouped[g] = h1_pool.tile([P, 4 * FEATURES], BF16, tag="h1", name="h1", align_bytes=64)
+            parts = products[pair][:].rearrange("p (e s d) -> p e s d", e=2, s=2)
             nc.scalar.copy(
-                out=h1gs[g][:].rearrange("p (d t) -> p d t", t=4)[:, :, 2 * u : 2 * u + 2],
+                out=h1_grouped[g][:].rearrange("p (d t) -> p d t", t=4)[:, :, 2 * u : 2 * u + 2],
                 in_=parts[:, :, 0, :].rearrange("p e d -> p d e"),
             )
 
-        def add_to_feat(j):
-            parts = hps[j][:].rearrange("p (e s d) -> p e s d", e=2, s=2)
-            fv = feat[:, 2 * j * D : (2 * j + 2) * D].rearrange("p (e d) -> p e d", e=2)
+        def add_products(pair):
+            parts = products[pair][:].rearrange("p (e s d) -> p e s d", e=2, s=2)
+            rows = feat[:, 2 * pair * FEATURES : (2 * pair + 2) * FEATURES].rearrange("p (e d) -> p e d", e=2)
             nc.vector.scalar_tensor_tensor(
-                out=fv, in0=parts[:, :, 0, :], scalar=w_f[:, 1:2], in1=fv, op0=ALU.mult, op1=ALU.add
+                out=rows, in0=parts[:, :, 0, :], scalar=w[:, 1:2], in1=rows, op0=ALU.mult, op1=ALU.add
             )
-            if avail(2 * j) > 0:
+            if h1_groups_ready(2 * pair) > 0:
                 nc.vector.scalar_tensor_tensor(
-                    out=fv, in0=parts[:, :, 1, :], scalar=w_f[:, 2:3], in1=fv, op0=ALU.mult, op1=ALU.add
+                    out=rows, in0=parts[:, :, 1, :], scalar=w[:, 2:3], in1=rows, op0=ALU.mult, op1=ALU.add
                 )
 
         def quantise_h1(g):
+            columns = slice(g * 2 * FEATURES + FEATURES, (g + 1) * 2 * FEATURES)
             nc.vector.quantize_mx(
-                out=xh_codes[:, g * 256 + 128 : g * 256 + 256].bitcast(FP8X4),
-                scales=xh_scales[:, g * 256 + 128 : g * 256 + 256],
-                in_=h1gs[g][:],
+                out=xh_codes[:, columns].bitcast(FP8X4), scales=xh_scales[:, columns], in_=h1_grouped[g][:]
             )
-            h1_ready[0] += 1
 
-        def transpose_bank(s):
-            rawf = raws[s // 8][:].bitcast(F32)
-            pt = tpp.tile([P, 512], F32, tag="tp", name="pt")
-            for q in range(4):
-                lo = (s % 8) * 512 + q * 128
-                nc.tensor.transpose(out=pt[:, q * 128 : (q + 1) * 128], in_=rawf[:, lo : lo + 128], identity=ident[:])
-            if s % 2 == 0:
-                grps[s // 2] = grpp.tile([P, 2048], BF16, tag="grp", name="grp", align_bytes=64)
-            dst = grps[s // 2][:].bitcast(F32)[:, (s % 2) * 512 : (s % 2 + 1) * 512].rearrange("p (c m u) -> p c m u", c=2, u=2)
-            src = pt[:].rearrange("p (c u m) -> p c m u", c=2, u=2)
-            if s % 4 == 3 and s % 16 != 15:
-                nc.vector.tensor_copy(out=dst, in_=src)
-            else:
-                nc.scalar.copy(out=dst, in_=src)
+        def hop2_passes(r, first_pass, last_pass):
+            g = r // 4
+            if g not in hop2:
+                if g < TRANSPOSE_BANKS:
+                    hop2[g] = transpose_psum.tile([P, BANK], F32, tag="bank", name="hop2")
+                else:
+                    hop2[g] = product_psum.tile([P, BANK], F32, tag="products", name="hop2")
+            for c in range(first_pass, last_pass + 1):
+                acc = hop2[g][:, (r % 4) * FEATURES : (r % 4 + 1) * FEATURES]
+                mx_pass(acc, r, c, FEATURES, FEATURES, c == h1_groups_ready(r))
 
-        nc.scalar.dma_start(out=w_bf[:], in_=w_p.rearrange("a b -> (a b)").partition_broadcast(P))
-        x_raw = rawp.tile([P, TILES * D], BF16, tag="raw", name="x_raw")
+        nc.scalar.dma_start(out=w_bf16[:], in_=w_p.rearrange("a b -> (a b)").partition_broadcast(P))
+        x_raw = raw_pool.tile([P, ROW_TILES * FEATURES], BF16, tag="raw", name="x_raw")
         nc.sync.dma_start(
-            out=x_raw[:].rearrange("p (j w) -> p j w", j=UNITS),
+            out=x_raw[:].rearrange("p (j w) -> p j w", j=PAIRS),
             in_=x_p.rearrange("(j m e) d -> m j (e d)", m=P, e=2),
         )
-        load(0)
-        load(1)
+        for r in range(RAW_TILES - 1):
+            load(r)
         masks.make_identity(nc, ident[:])
-        nc.vector.tensor_copy(out=w_f[:], in_=w_bf[:])
-        xgs = []
-        for h in range(2):
-            xg = grpp.tile([P, 2048], BF16, tag="grp", name="xg", align_bytes=64)
-            xgs.append(xg)
+        nc.vector.tensor_copy(out=w[:], in_=w_bf16[:])
+        x_grouped = []
+        for half in range(2):
+            x_half = grouped_pool.tile([P, 4 * BANK], BF16, tag="grouped", name="x_half", align_bytes=64)
+            x_grouped.append(x_half)
             nc.vector.tensor_copy(
-                out=xg[:].rearrange("p (c d t) -> p c d t", c=4, t=4),
-                in_=x_raw[:, h * 2048 : (h + 1) * 2048].rearrange("p (c t d) -> p c d t", c=4, t=4),
+                out=x_half[:].rearrange("p (c d t) -> p c d t", c=4, t=4),
+                in_=x_raw[:, half * 4 * BANK : (half + 1) * 4 * BANK].rearrange("p (c t d) -> p c d t", c=4, t=4),
             )
         for c in range(PASSES):
+            columns = slice(c * 2 * FEATURES, c * 2 * FEATURES + FEATURES)
             nc.vector.quantize_mx(
-                out=xh_codes[:, c * 256 : c * 256 + 128].bitcast(FP8X4),
-                scales=xh_scales[:, c * 256 : c * 256 + 128],
-                in_=xgs[c // 4][:, (c % 4) * 512 : (c % 4 + 1) * 512],
+                out=xh_codes[:, columns].bitcast(FP8X4),
+                scales=xh_scales[:, columns],
+                in_=x_grouped[c // 4][:, (c % 4) * BANK : (c % 4 + 1) * BANK],
             )
-        for h in range(4):
-            nc.scalar.activation(
-                out=feat[:, h * 1024 : (h + 1) * 1024],
-                in_=x_raw[:, h * 1024 : (h + 1) * 1024],
-                func=ACT.Copy,
-                scale=w_f[:, 0:1],
-            )
+        for quarter in range(4):
+            columns = slice(quarter * 2 * BANK, (quarter + 1) * 2 * BANK)
+            nc.scalar.activation(out=feat[:, columns], in_=x_raw[:, columns], func=ACT.Copy, scale=w[:, 0:1])
 
-        for s in range(BANKS):
-            if s % 8 == 0 and s // 8 + 2 < UNITS:
-                load(s // 8 + 2)
-            transpose_bank(s)
-            if s % 2 == 1 and s >= 3:
-                quantise_a(s // 2 - 1)
-            if s in evacuate_at:
-                round_h1(evacuate_at[s])
-                add_to_feat(evacuate_at[s])
-            if s in quantise_h1_at:
-                quantise_h1(quantise_h1_at[s])
-            if (s + 1) % RUN == 0 or s == BANKS - 1:
-                before = issued[0]
-                hop1_passes(2 * (s + 1) - LAG)
-                if issued[0] // 16 > before // 16:
-                    j = issued[0] // 16 - 1
-                    evacuate_at[s + 2] = j
-                    if j % 2 == 1:
-                        quantise_h1_at[s + 4] = j // 2
-        quantise_a(BANKS // 2 - 1)
+        for r in range(ROW_TILES):
+            if r + RAW_TILES - 1 < ROW_TILES:
+                load(r + RAW_TILES - 1)
+            transposes(r)
+            if r >= 2:
+                hop1(r - 2)
+        quantise_a(ROW_TILES - 1, 1)
 
-        tails = {}
-
-        def tail_passes(g, t, first, final):
-            if g not in tails:
-                if g < 6:
-                    tails[g] = tpp.tile([P, 512], F32, tag="tp", name="tl")
-                else:
-                    tails[g] = hpp.tile([P, 512], F32, tag="hp", name="tl")
-            r = 4 * g + t
-            for c in range(first, final + 1):
-                mx_pass(tails[g][:, t * 128 : (t + 1) * 128], r, c, 128, 128, c == avail(r))
-
-        round_h1(UNITS - 2)
-        add_to_feat(UNITS - 2)
-        hop1_passes((TILES - 1) * PASSES)
-        for g in (0, 1, 2):
-            tail_passes(g, 0, avail(4 * g), PASSES - 2)
-        hop1_passes(TILES * PASSES)
-        for g in (3, 4, 5):
-            tail_passes(g, 0, avail(4 * g), PASSES - 2)
-        round_h1(UNITS - 1)
+        round_h1(PAIRS - 2)
+        add_products(PAIRS - 2)
+        hop1(ROW_TILES - 2)
+        for g in range(TRANSPOSE_BANKS // 2):
+            hop2_passes(4 * g, h1_groups_ready(4 * g), PASSES - 2)
+        hop1(ROW_TILES - 1)
+        for g in range(TRANSPOSE_BANKS // 2, TRANSPOSE_BANKS):
+            hop2_passes(4 * g, h1_groups_ready(4 * g), PASSES - 2)
+        round_h1(PAIRS - 1)
         quantise_h1(PASSES - 1)
-        add_to_feat(UNITS - 1)
+        add_products(PAIRS - 1)
         for g in range(PASSES):
-            for t in range(4):
-                if t == 0 and g < 6:
-                    tail_passes(g, 0, PASSES - 1, PASSES - 1)
+            for r in range(4 * g, 4 * g + 4):
+                if r % 4 == 0 and g < TRANSPOSE_BANKS:
+                    hop2_passes(r, PASSES - 1, PASSES - 1)
                 else:
-                    tail_passes(g, t, avail(4 * g + t), PASSES - 1)
-            fv = feat[:, g * 512 : (g + 1) * 512]
+                    hop2_passes(r, h1_groups_ready(r), PASSES - 1)
+            rows = feat[:, g * BANK : (g + 1) * BANK]
             nc.vector.scalar_tensor_tensor(
-                out=fv, in0=tails[g][:], scalar=w_f[:, 2:3], in1=fv, op0=ALU.mult, op1=ALU.add
+                out=rows, in0=hop2[g][:], scalar=w[:, 2:3], in1=rows, op0=ALU.mult, op1=ALU.add
             )
-            nc.sync.dma_start(out=out_groups[g], in_=fv.rearrange("p (u w) -> p u w", u=2))
+            nc.sync.dma_start(out=out_groups[g], in_=rows.rearrange("p (u w) -> p u w", u=2))

from contextlib import ExitStack

import concourse.masks as masks
import concourse.mybir as mybir

F32 = mybir.dt.float32
BF16 = mybir.dt.bfloat16
U32 = mybir.dt.uint32
U8 = mybir.dt.uint8
FP8X4 = mybir.dt.float8_e4m3fn_x4
ALU = mybir.AluOpType
ACT = mybir.ActivationFunctionType

P = 128
NODES = 4096
FEATURES = 128
PASSES = NODES // (4 * P)
ROW_TILES = NODES // P
PAIRS = ROW_TILES // 2
BANK = 512
TILE_WORDS = PASSES * P
TRANSPOSE_BANKS = 6
RAW_TILES = 6
FLOPS = 2 * 2 * NODES * NODES * FEATURES


def h1_groups_ready(r):
    return max(0, (r - 2) // 4)


def tile_simpa_pb_t_kernel(tc, A_p, x_p, w_p, out):
    nc = tc.nc
    a_row_tiles = A_p.rearrange("(j m e) k -> j e m k", m=P, e=2)
    out_groups = out.rearrange("(g u m e) d -> g m u (e d)", u=2, m=P, e=2)

    with ExitStack() as ctx:
        keep = ctx.enter_context(tc.tile_pool(name="keep", bufs=1))
        raw_pool = ctx.enter_context(tc.tile_pool(name="raw_pool", bufs=RAW_TILES))
        grouped_pool = ctx.enter_context(tc.tile_pool(name="grouped_pool", bufs=4))
        h1_pool = ctx.enter_context(tc.tile_pool(name="h1_pool", bufs=2))
        transpose_psum = ctx.enter_context(tc.psum_pool(name="transpose_psum", bufs=TRANSPOSE_BANKS))
        product_psum = ctx.enter_context(tc.psum_pool(name="product_psum", bufs=2))
        ctx.enter_context(tc.manual_schedule())

        a_codes = keep.tile([P, ROW_TILES * TILE_WORDS], U32, name="a_codes", align_bytes=64)
        a_scales = keep.tile([P, ROW_TILES // 4 * TILE_WORDS], U8, name="a_scales", align_bytes=64)
        xh_codes = keep.tile([P, PASSES * 2 * FEATURES], U32, name="xh_codes", align_bytes=64)
        xh_scales = keep.tile([P, PASSES * 2 * FEATURES], U8, name="xh_scales", align_bytes=64)
        feat = keep.tile([P, ROW_TILES * FEATURES], F32, name="feat")
        ident = keep.tile([P, P], F32, name="ident")
        w_bf16 = keep.tile([P, 3], BF16, name="w_bf16")
        w = keep.tile([P, 3], F32, name="w")

        raw = {}
        grouped = {}
        products = {}
        h1_grouped = {}
        hop2 = {}

        def a_plane(r, first, width):
            g = r // 4
            columns = ((g // 4) * 4 + r % 4) * TILE_WORDS + first
            return a_scales[4 * (g % 4) : P, columns : columns + width]

        def load(r):
            raw[r] = raw_pool.tile([P, NODES], BF16, tag="raw", name="raw")
            nc.sync.dma_start(out=raw[r][:], in_=a_row_tiles[r // 2][r % 2])

        def quantise_a(r, half):
            first = half * (TILE_WORDS // 2)
            nc.vector.quantize_mx(
                out=a_codes[:, r * TILE_WORDS + first : r * TILE_WORDS + first + TILE_WORDS // 2].bitcast(FP8X4),
                scales=a_plane(r, first, TILE_WORDS // 2),
                in_=grouped[(r, half)][:],
            )

        def mx_pass(acc, r, c, first, width, start):
            moving = slice(c * 2 * FEATURES + first, c * 2 * FEATURES + first + width)
            nc.tensor.matmul_mx(
                out=acc,
                lhsT=a_codes[:, r * TILE_WORDS + c * P : r * TILE_WORDS + (c + 1) * P].bitcast(FP8X4),
                lhsT_scale=a_plane(r, c * P, P),
                rhs=xh_codes[:, moving].bitcast(FP8X4),
                rhs_scale=xh_scales[:, moving],
                start=start,
                stop=(c == PASSES - 1),
            )

        def transposes(r):
            words = raw[r][:].bitcast(F32)
            for b in range(4):
                bank = transpose_psum.tile([P, BANK], F32, tag="bank", name="bank")
                for q in range(4):
                    nc.tensor.transpose(
                        out=bank[:, q * P : (q + 1) * P],
                        in_=words[:, (4 * b + q) * P : (4 * b + q + 1) * P],
                        identity=ident[:],
                    )
                half = b // 2
                if b % 2 == 0:
                    grouped[(r, half)] = grouped_pool.tile([P, 4 * BANK], BF16, tag="grouped", name="grouped", align_bytes=64)
                target = grouped[(r, half)][:].bitcast(F32)[:, (b % 2) * BANK : (b % 2 + 1) * BANK]
                target = target.rearrange("p (c m u) -> p c m u", c=2, u=2)
                source = bank[:].rearrange("p (c u m) -> p c m u", c=2, u=2)
                if b == 3 and r % 4 != 3:
                    nc.vector.tensor_copy(out=target, in_=source)
                else:
                    nc.scalar.copy(out=target, in_=source)
                if b == 1 and r > 0:
                    quantise_a(r - 1, 1)
                if b == 3:
                    quantise_a(r, 0)
                if b == 1 and r % 2 == 0 and r >= 4:
                    round_h1((r - 4) // 2)
                    add_products((r - 4) // 2)
                if b == 3 and r % 4 == 2 and r >= 6:
                    quantise_h1((r - 6) // 4)

        def hop1(r):
            if r % 2 == 0:
                products[r // 2] = product_psum.tile([P, BANK], F32, tag="products", name="products")
            for c in range(PASSES):
                width = 2 * FEATURES if c < h1_groups_ready(r) else FEATURES
                first = (r % 2) * 2 * FEATURES
                mx_pass(products[r // 2][:, first : first + width], r, c, 0, width, c == 0)

        def round_h1(pair):
            g = pair // 2
            u = pair % 2
            if u == 0:
                h1_grouped[g] = h1_pool.tile([P, 4 * FEATURES], BF16, tag="h1", name="h1", align_bytes=64)
            parts = products[pair][:].rearrange("p (e s d) -> p e s d", e=2, s=2)
            nc.scalar.copy(
                out=h1_grouped[g][:].rearrange("p (d t) -> p d t", t=4)[:, :, 2 * u : 2 * u + 2],
                in_=parts[:, :, 0, :].rearrange("p e d -> p d e"),
            )

        def add_products(pair):
            parts = products[pair][:].rearrange("p (e s d) -> p e s d", e=2, s=2)
            rows = feat[:, 2 * pair * FEATURES : (2 * pair + 2) * FEATURES].rearrange("p (e d) -> p e d", e=2)
            nc.vector.scalar_tensor_tensor(
                out=rows, in0=parts[:, :, 0, :], scalar=w[:, 1:2], in1=rows, op0=ALU.mult, op1=ALU.add
            )
            if h1_groups_ready(2 * pair) > 0:
                nc.vector.scalar_tensor_tensor(
                    out=rows, in0=parts[:, :, 1, :], scalar=w[:, 2:3], in1=rows, op0=ALU.mult, op1=ALU.add
                )

        def quantise_h1(g):
            columns = slice(g * 2 * FEATURES + FEATURES, (g + 1) * 2 * FEATURES)
            nc.vector.quantize_mx(
                out=xh_codes[:, columns].bitcast(FP8X4), scales=xh_scales[:, columns], in_=h1_grouped[g][:]
            )

        def hop2_passes(r, first_pass, last_pass):
            g = r // 4
            if g not in hop2:
                if g < TRANSPOSE_BANKS:
                    hop2[g] = transpose_psum.tile([P, BANK], F32, tag="bank", name="hop2")
                else:
                    hop2[g] = product_psum.tile([P, BANK], F32, tag="products", name="hop2")
            for c in range(first_pass, last_pass + 1):
                acc = hop2[g][:, (r % 4) * FEATURES : (r % 4 + 1) * FEATURES]
                mx_pass(acc, r, c, FEATURES, FEATURES, c == h1_groups_ready(r))

        nc.scalar.dma_start(out=w_bf16[:], in_=w_p.rearrange("a b -> (a b)").partition_broadcast(P))
        x_raw = raw_pool.tile([P, ROW_TILES * FEATURES], BF16, tag="raw", name="x_raw")
        nc.sync.dma_start(
            out=x_raw[:].rearrange("p (j w) -> p j w", j=PAIRS),
            in_=x_p.rearrange("(j m e) d -> m j (e d)", m=P, e=2),
        )
        for r in range(RAW_TILES - 1):
            load(r)
        masks.make_identity(nc, ident[:])
        nc.vector.tensor_copy(out=w[:], in_=w_bf16[:])
        x_grouped = []
        for half in range(2):
            x_half = grouped_pool.tile([P, 4 * BANK], BF16, tag="grouped", name="x_half", align_bytes=64)
            x_grouped.append(x_half)
            nc.vector.tensor_copy(
                out=x_half[:].rearrange("p (c d t) -> p c d t", c=4, t=4),
                in_=x_raw[:, half * 4 * BANK : (half + 1) * 4 * BANK].rearrange("p (c t d) -> p c d t", c=4, t=4),
            )
        for c in range(PASSES):
            columns = slice(c * 2 * FEATURES, c * 2 * FEATURES + FEATURES)
            nc.vector.quantize_mx(
                out=xh_codes[:, columns].bitcast(FP8X4),
                scales=xh_scales[:, columns],
                in_=x_grouped[c // 4][:, (c % 4) * BANK : (c % 4 + 1) * BANK],
            )
        for quarter in range(4):
            columns = slice(quarter * 2 * BANK, (quarter + 1) * 2 * BANK)
            nc.scalar.activation(out=feat[:, columns], in_=x_raw[:, columns], func=ACT.Copy, scale=w[:, 0:1])

        for r in range(ROW_TILES):
            if r + RAW_TILES - 1 < ROW_TILES:
                load(r + RAW_TILES - 1)
            transposes(r)
            if r >= 2:
                hop1(r - 2)
        quantise_a(ROW_TILES - 1, 1)

        round_h1(PAIRS - 2)
        add_products(PAIRS - 2)
        hop1(ROW_TILES - 2)
        for g in range(TRANSPOSE_BANKS // 2):
            hop2_passes(4 * g, h1_groups_ready(4 * g), PASSES - 2)
        hop1(ROW_TILES - 1)
        for g in range(TRANSPOSE_BANKS // 2, TRANSPOSE_BANKS):
            hop2_passes(4 * g, h1_groups_ready(4 * g), PASSES - 2)
        round_h1(PAIRS - 1)
        quantise_h1(PASSES - 1)
        add_products(PAIRS - 1)
        for g in range(PASSES):
            for r in range(4 * g, 4 * g + 4):
                if r % 4 == 0 and g < TRANSPOSE_BANKS:
                    hop2_passes(r, PASSES - 1, PASSES - 1)
                else:
                    hop2_passes(r, h1_groups_ready(r), PASSES - 1)
            rows = feat[:, g * BANK : (g + 1) * BANK]
            nc.vector.scalar_tensor_tensor(
                out=rows, in0=hop2[g][:], scalar=w[:, 2:3], in1=rows, op0=ALU.mult, op1=ALU.add
            )
            nc.sync.dma_start(out=out_groups[g], in_=rows.rearrange("p (u w) -> p u w", u=2))
